import numpy as np
import ml_dtypes


def mxq(x, axis, fmt="e4m3"):
    dtype, down = {"e4m3": (ml_dtypes.float8_e4m3fn, 7), "e5m2": (ml_dtypes.float8_e5m2, 14)}[fmt]
    v = np.moveaxis(np.asarray(x, np.float32).astype(ml_dtypes.bfloat16).astype(np.float64), axis, -1)
    blocks = v.reshape(v.shape[:-1] + (-1, 32))
    amax = np.abs(blocks).max(-1, keepdims=True)
    byte = np.maximum(np.where(amax > 0, np.frexp(amax)[1] - 1 + 127, 0) - down, 1)
    scale = np.exp2(byte - 127.0)
    codes = (blocks / scale).astype(np.float32).astype(dtype).astype(np.float64)
    return np.moveaxis((codes * scale).reshape(v.shape), -1, axis)


WIDE = False


def mx_kscale(k, group=512):
    if not WIDE:
        return np.ones(k)
    levels = np.array([18, -18])
    if group != 512:
        return np.exp2(np.random.permutation(np.resize(levels, k // group))).repeat(group)
    if k % 512:
        return np.exp2(np.random.permutation(np.resize(levels, k // 32))).repeat(32)
    a = np.empty((k // 512, 16))
    for p in range(k // 512):
        a[p, :8] = np.random.permutation(np.resize(levels, 8))
        for g in range(8):
            far = levels[np.abs(levels - a[p, g]) >= 10]
            a[p, g + 8] = far[np.random.randint(len(far))]
    return np.exp2(a.ravel()).repeat(32)


BF16 = ml_dtypes.bfloat16


def bf(x):
    return np.asarray(x, np.float32).astype(BF16)


def f64(x):
    return np.asarray(x).astype(np.float64)


B, T, DETER, G = 4, 256, 1024, 2
N = B * T
BH = DETER // G


def silu(v):
    return v / (1.0 + np.exp(-v))


def sigmoid(v):
    return 1.0 / (1.0 + np.exp(-v))


def gate_values(h, W_gate, b_gate):
    hb = f64(h).reshape(N, G, BH).transpose(1, 0, 2)
    return (hb @ f64(W_gate) + f64(b_gate)[:, None, :]).transpose(1, 0, 2)


def setup_inputs():
    s = mx_kscale(N)
    u = mx_kscale(DETER, 128)
    h0 = bf(silu(np.random.standard_normal((N, DETER))))
    d = bf(np.random.standard_normal((B, T, DETER)))
    W0 = bf(np.random.standard_normal((G, BH, 3 * BH)) * 2.0 / np.sqrt(BH))
    b_gate = bf(0.3 * np.random.standard_normal((G, 3 * BH)))
    noise = np.random.standard_normal((B, T, DETER)) * np.exp2(np.random.randint(-6, 1, (B, T, 1)))
    g = bf(4.0 * noise / s.reshape(B, T, 1) * u)
    gates = gate_values(h0, W0, b_gate)
    uw = np.tile(u.reshape(G, BH), (1, 3))[:, None, :]
    return {
        "h": bf(f64(h0) * s[:, None]),
        "d": d,
        "W_gate": bf(f64(W0) / uw),
        "b_gate": b_gate,
        "gates": np.asarray(gates, np.float32),
        "grad_out": g,
    }


def reference(h, d, W_gate, b_gate, gates, grad_out):
    zf = f64(gates)
    r = sigmoid(zf[:, :, :BH])
    up = sigmoid(zf[:, :, BH:2 * BH] - 1.0)
    c = zf[:, :, 2 * BH:]
    cand = np.tanh(r * c)
    g = f64(grad_out).reshape(N, G, BH)
    d2 = f64(d).reshape(N, G, BH)
    dp = g * up * (1.0 - cand * cand)
    dr = dp * c * r * (1.0 - r)
    du = g * (cand - d2) * up * (1.0 - up)
    dc = dp * r
    dz = np.concatenate([dr, du, dc], axis=-1).transpose(1, 0, 2)
    wq = mxq(f64(W_gate), 2, "e4m3")
    dh = mxq(dz, 2, "e5m2") @ wq.transpose(0, 2, 1)
    hq = mxq(f64(h).reshape(N, G, BH).transpose(1, 0, 2), 1, "e4m3")
    dw = hq.transpose(0, 2, 1) @ mxq(dz, 1, "e5m2")
    return dh.transpose(1, 0, 2).reshape(N, DETER), dw

@@ -1,0 +1,352 @@
+from contextlib import ExitStack
+
+import concourse.mybir as mybir
+from concourse.masks import make_identity
+
+TOKENS, FEATURES, BLOCKS = 1024, 1024, 2
+BH = FEATURES // BLOCKS
+GATES = 3 * BH
+
+FLOPS = 2 * (2 * TOKENS * BLOCKS * BH * GATES)
+BYTES = 2 * (3 * TOKENS * FEATURES + BLOCKS * BH * GATES) + 4 * (
+    TOKENS * BLOCKS * GATES + TOKENS * FEATURES + BLOCKS * BH * GATES
+)
+
+F32 = mybir.dt.float32
+BF16 = mybir.dt.bfloat16
+U32 = mybir.dt.uint32
+U8 = mybir.dt.uint8
+E4M3 = mybir.dt.float8_e4m3fn_x4
+E5M2 = mybir.dt.float8_e5m2_x4
+ALU = mybir.AluOpType
+ACT = mybir.ActivationFunctionType
+
+P = 128
+PACK = 4
+K_PASS = P * PACK
+HALF = BH // 2
+R, U, C = 0, 1, 2
+
+
+def tile_blockrecurrentmodel_pb_v_kernel(tc, h, d, w_gate, b_gate, gates, grad_out, out_0, out_1):
+    nc = tc.nc
+    d = d.flatten_outer_dims()
+    grad_out = grad_out.flatten_outer_dims()
+    chunks = [(g, t) for g in range(BLOCKS) for t in range(TOKENS // K_PASS)]
+
+    with ExitStack() as ctx:
+        const = ctx.enter_context(tc.tile_pool(name="const", bufs=1))
+        stream = ctx.enter_context(tc.tile_pool(name="stream", bufs=2))
+        work = ctx.enter_context(tc.tile_pool(name="work", bufs=1))
+        group = ctx.enter_context(tc.tile_pool(name="group", bufs=3))
+        tcode = ctx.enter_context(tc.tile_pool(name="tcode", bufs=8))
+        fcode = ctx.enter_context(tc.tile_pool(name="fcode", bufs=4))
+        stage = ctx.enter_context(tc.tile_pool(name="stage", bufs=6))
+        psum = ctx.enter_context(tc.psum_pool(name="psum", bufs=4))
+        ctx.enter_context(tc.manual_schedule())
+
+        minus_one = const.tile([P, 1], F32, name="minus_one")
+        nc.vector.memset(minus_one[:], -1.0)
+        warm = const.tile([P, 1], F32, name="warm")
+        nc.scalar.activation(warm[:], minus_one[:], ACT.Sigmoid)
+        ident = const.tile([P, P], F32, name="ident")
+        make_identity(nc, ident[:])
+
+        w_codes = const.tile([P, BLOCKS, 3, BH], U32, name="w_codes", align_bytes=64)
+        w_scales = const.tile([P, BLOCKS, 3, BH], U8, name="w_scales", align_bytes=64)
+        h_codes = const.tile([P, 2, FEATURES], U32, name="h_codes", align_bytes=64)
+        h_scales = const.tile([P, 2, FEATURES], U8, name="h_scales", align_bytes=64)
+
+        gate_in, g_in, d_in, w_in = {}, {}, {}, {}
+        cand_t, q_t, a_t, dz = {}, {}, {}, {}
+        tok, feat, grouped = {}, {}, {}
+
+        def rows(t):
+            return slice(K_PASS * t, K_PASS * (t + 1))
+
+        def load_chunk(i, pieces):
+            g, t = chunks[i]
+            for s, nm in ((R, "r_in"), (C, "c_in"), (U, "u_in")):
+                gate_in[i, s] = stream.tile([P, PACK, BH], F32, name=nm)
+            g_in[i] = stream.tile([P, PACK, BH], BF16, name="g_in")
+            d_in[i] = stream.tile([P, PACK, BH], BF16, name="d_in")
+            width = BH // pieces
+            for q in range(pieces):
+                ws = slice(q * width, (q + 1) * width)
+                for s in (R, C):
+                    src = gates[rows(t), g, s * BH + q * width : s * BH + (q + 1) * width]
+                    nc.sync.dma_start(out=gate_in[i, s][:, :, ws], in_=src.rearrange("(p j) w -> p j w", j=PACK))
+            src = gates[rows(t), g, U * BH : (U + 1) * BH]
+            nc.sync.dma_start(out=gate_in[i, U][:], in_=src.rearrange("(p j) w -> p j w", j=PACK))
+            cols = slice(g * BH, (g + 1) * BH)
+            nc.sync.dma_start(out=g_in[i][:], in_=grad_out[rows(t), cols].rearrange("(p j) w -> p j w", j=PACK))
+            nc.sync.dma_start(out=d_in[i][:], in_=d[rows(t), cols].rearrange("(p j) w -> p j w", j=PACK))
+
+        def load_w(g):
+            w_in[g] = work.tile([P, BH // P, GATES], BF16, name="w_in", align_bytes=64)
+            nc.sync.dma_start(out=w_in[g][:], in_=w_gate[g].rearrange("(b p) k -> p b k", p=P))
+
+        def load_h(g, t):
+            raw = stream.tile([P, PACK, BH], BF16, name="h_in")
+            w_in["h", g, t] = raw
+            nc.sync.dma_start(
+                out=raw[:], in_=h[rows(t), g * BH : (g + 1) * BH].rearrange("(p j) w -> p j w", j=PACK)
+            )
+
+        def half(a, x):
+            return a[:, :, x * HALF : (x + 1) * HALF]
+
+        def sig(i):
+            for s, bias in ((R, 0.0), (U, minus_one[:])):
+                for x in (0, 1):
+                    v = half(gate_in[i, s], x)
+                    nc.scalar.activation(v, v, ACT.Sigmoid, bias=bias)
+
+        def work_tiles(i):
+            cand_t[i] = work.tile([P, PACK, BH], F32, name="cand")
+            q_t[i] = work.tile([P, PACK, BH], F32, name="q")
+            a_t[i] = work.tile([P, PACK, BH], F32, name="a")
+            dz[i, R] = work.tile([P, BH, PACK], BF16, name="dr", align_bytes=64)
+            dz[i, U] = work.tile([P, BH, PACK], BF16, name="du", align_bytes=64)
+            dz[i, C] = work.tile([P, BH, PACK], BF16, name="dc", align_bytes=64)
+
+        def stt(out, in0, scalar, op0, in1):
+            nc.vector.scalar_tensor_tensor(out=out, in0=in0, scalar=scalar, in1=in1, op0=op0, op1=ALU.mult)
+
+        def v_m(i, x):
+            c = half(gate_in[i, C], x)
+            stt(c, half(gate_in[i, R], x), -1.0, ALU.mult, c)
+
+        def v_a(i, x):
+            stt(half(a_t[i], x), half(g_in[i], x), -1.0, ALU.mult, half(gate_in[i, U], x))
+
+        def v_b(i, x):
+            u = half(gate_in[i, U], x)
+            stt(u, u, -1.0, ALU.add, half(a_t[i], x))
+
+        def v_w(i, x):
+            m = half(gate_in[i, C], x)
+            stt(m, half(gate_in[i, R], x), -1.0, ALU.add, m)
+
+        def v_e(i, x):
+            e = half(cand_t[i], x)
+            nc.vector.tensor_tensor(out=e, in0=e, in1=half(d_in[i], x), op=ALU.subtract)
+
+        def v_dp(i, x):
+            q = half(q_t[i], x)
+            stt(q, q, -1.0, ALU.add, half(a_t[i], x))
+
+        def v_dz(i, s, x):
+            in0, in1 = {
+                R: (gate_in[i, C], q_t[i]),
+                U: (gate_in[i, U], cand_t[i]),
+                C: (q_t[i], gate_in[i, R]),
+            }[s]
+            view = "p j (c i) -> p c j i"
+            nc.vector.tensor_tensor(
+                out=dz[i, s][:, x * HALF : (x + 1) * HALF, :].rearrange("p (c i) j -> p c j i", i=4),
+                in0=half(in0, x).rearrange(view, i=4),
+                in1=half(in1, x).rearrange(view, i=4),
+                op=ALU.mult,
+            )
+
+        def s_tanh(i):
+            for x in (0, 1):
+                nc.scalar.activation(half(cand_t[i], x), half(gate_in[i, C], x), ACT.Tanh, scale=-1.0)
+
+        def s_square(i):
+            for x in (0, 1):
+                nc.scalar.activation(half(q_t[i], x), half(cand_t[i], x), ACT.Square)
+
+        def quant_tok(i, s):
+            codes = tcode.tile([P, BH], U32, name="tok_codes", align_bytes=64)
+            scales = tcode.tile([P, BH], U8, name="tok_scales", align_bytes=64)
+            tok[i, s] = (codes, scales)
+            nc.vector.quantize_mx(
+                out=codes[:].bitcast(E5M2), scales=scales[:], in_=dz[i, s][:].rearrange("p w j -> p (w j)")
+            )
+
+        def turn(i, s):
+            words = dz[i, s][:].rearrange("p w j -> p (w j)").bitcast(F32)
+            grp = group.tile([P, 2, 2, P, PACK], BF16, name="feat_grp", align_bytes=64)
+            grouped[i, s] = grp
+            for u in (0, 1):
+                xt = psum.tile([P, PACK, P], F32, name="xt")
+                for t in range(PACK):
+                    nc.tensor.transpose(xt[:, t, :], words[:, 2 * t + u : 2 * BH : 8], ident[:])
+                src = xt[:].rearrange("p t q -> p (t q)").bitcast(BF16)
+                nc.scalar.copy(out=grp[:, u], in_=src.rearrange("p (t q e) -> p e q t", t=PACK, e=2))
+
+        def quant_feat(i, s):
+            codes = fcode.tile([P, K_PASS], U32, name="feat_codes", align_bytes=64)
+            scales = fcode.tile([P, K_PASS], U8, name="feat_scales", align_bytes=64)
+            feat[i, s] = (codes, scales)
+            nc.vector.quantize_mx(
+                out=codes[:].bitcast(E5M2),
+                scales=scales[:],
+                in_=grouped[i, s][:].rearrange("p u e q t -> p (u e q t)"),
+            )
+
+        def turn_w(g, s):
+            grp = group.tile([P, BH // P, P, 2, 2], BF16, name="wh_grp", align_bytes=64)
+            grouped["w", g, s] = grp
+            words = [w_in[g][:, b, :].bitcast(F32) for b in range(BH // P)]
+            dst = grp[:].rearrange("p b o u e -> p (b o u e)").bitcast(F32)
+            for b2 in (0, 1):
+                xt = psum.tile([P, PACK, P], F32, name="xt")
+                for k in range(4):
+                    b, u = 2 * b2 + k // 2, k % 2
+                    nc.tensor.transpose(xt[:, k, :], words[b][:, 256 * s + u : 256 * (s + 1) : 2], ident[:])
+                nc.scalar.copy(
+                    out=dst[:, 512 * b2 : 512 * (b2 + 1)].rearrange("p (b o u) -> p b o u", b=2, u=2),
+                    in_=xt[:].rearrange("p (b u) o -> p b o u", u=2),
+                )
+
+        def quant_w(g, s):
+            nc.vector.quantize_mx(
+                out=w_codes[:, g, s, :].bitcast(E4M3),
+                scales=w_scales[:, g, s, :],
+                in_=grouped["w", g, s][:].rearrange("p b o u e -> p (b o u e)"),
+            )
+
+        def group_h(g, t):
+            grp = group.tile([P, BH, PACK], BF16, name="wh_grp", align_bytes=64)
+            grouped["h", g, t] = grp
+            nc.scalar.copy(
+                out=grp[:].rearrange("p (c i) j -> p c j i", i=4),
+                in_=w_in["h", g, t][:].rearrange("p j (c i) -> p c j i", i=4),
+            )
+
+        def quant_h(g, t):
+            cols = slice(g * BH, (g + 1) * BH)
+            nc.vector.quantize_mx(
+                out=h_codes[:, t, cols].bitcast(E4M3),
+                scales=h_scales[:, t, cols],
+                in_=grouped["h", g, t][:].rearrange("p w j -> p (w j)"),
+            )
+
+        def drain(acc, dst, on_vector):
+            res = stage.tile([P, BH], F32, name="res")
+            if on_vector:
+                nc.vector.tensor_copy(out=res[:], in_=acc[:])
+            else:
+                nc.scalar.copy(out=res[:], in_=acc[:])
+            nc.sync.dma_start(out=dst, in_=res[:])
+
+        def product_h(i, split):
+            g, t = chunks[i]
+            dst = out_0[rows(t), g * BH : (g + 1) * BH].rearrange("(p j) w -> p j w", j=PACK)
+            for j in range(PACK):
+                acc = psum.tile([P, BH], F32, name="acc")
+                for n, s in enumerate((U, C, R)):
+                    codes, scales = feat[i, s]
+                    nc.tensor.matmul_mx(
+                        out=acc[:],
+                        lhsT=codes[:, j * P : (j + 1) * P].bitcast(E5M2),
+                        lhsT_scale=scales[:, j * P : (j + 1) * P],
+                        rhs=w_codes[:, g, s, :].bitcast(E4M3),
+                        rhs_scale=w_scales[:, g, s, :],
+                        start=n == 0,
+                        stop=n == 2,
+                    )
+                drain(acc, dst[:, j, :], split and j % 2 == 0)
+
+        def product_w(g, s, split):
+            for m in range(BH // P):
+                acc = psum.tile([P, BH], F32, name="acc")
+                cols = slice(g * BH + m * P, g * BH + (m + 1) * P)
+                for t in (0, 1):
+                    codes, scales = tok[2 * g + t, s]
+                    nc.tensor.matmul_mx(
+                        out=acc[:],
+                        lhsT=h_codes[:, t, cols].bitcast(E4M3),
+                        lhsT_scale=h_scales[:, t, cols],
+                        rhs=codes[:].bitcast(E5M2),
+                        rhs_scale=scales[:],
+                        start=t == 0,
+                        stop=t == 1,
+                    )
+                drain(acc, out_1[g, m * P : (m + 1) * P, s * BH : (s + 1) * BH], split and m % 2 == 0)
+
+        load_chunk(0, 2)
+        load_w(0)
+        load_h(0, 0)
+        sig(0)
+        for i in range(4):
+            prev = i - 1
+            work_tiles(i)
+            if i + 1 < 4:
+                load_chunk(i + 1, 1)
+            if i == 0:
+                load_h(0, 1)
+            elif i == 1:
+                load_w(1)
+                load_h(1, 0)
+            elif i == 2:
+                load_h(1, 1)
+
+            v_m(i, 0)
+            if prev >= 0:
+                quant_tok(prev, R)
+            v_m(i, 1)
+            s_tanh(i)
+            s_square(i)
+            if prev >= 0:
+                quant_feat(prev, C)
+            v_a(i, 0)
+            v_a(i, 1)
+            v_b(i, 0)
+            if prev >= 0:
+                quant_feat(prev, R)
+            v_b(i, 1)
+            if prev >= 0:
+                product_h(prev, False)
+            if i == 0:
+                for s in range(3):
+                    turn_w(0, s)
+            v_e(i, 0)
+            v_e(i, 1)
+            v_dz(i, U, 0)
+            v_dz(i, U, 1)
+            turn(i, U)
+            if i + 1 < 4:
+                sig(i + 1)
+            if i == 0:
+                group_h(0, 0)
+            elif i == 1:
+                group_h(0, 1)
+                for s in range(3):
+                    turn_w(1, s)
+            elif i == 2:
+                group_h(1, 0)
+                for s in range(3):
+                    product_w(0, s, False)
+            else:
+                group_h(1, 1)
+            v_w(i, 0)
+            quant_tok(i, U)
+            v_w(i, 1)
+            if i == 0:
+                for s in range(3):
+                    quant_w(0, s)
+            v_dp(i, 0)
+            v_dp(i, 1)
+            v_dz(i, C, 0)
+            quant_feat(i, U)
+            v_dz(i, C, 1)
+            turn(i, C)
+            if i == 1:
+                for s in range(3):
+                    quant_w(1, s)
+            v_dz(i, R, 0)
+            quant_tok(i, C)
+            quant_h(*((0, 0), (0, 1), (1, 0), (1, 1))[i])
+            v_dz(i, R, 1)
+            turn(i, R)
+        product_w(1, U, False)
+        quant_tok(3, R)
+        quant_feat(3, C)
+        product_w(1, C, True)
+        quant_feat(3, R)
+        product_w(1, R, True)
+        product_h(3, True)

@@ -41,9 +41,9 @@ def tile_blockrecurrentmodel_pb_v_kernel(tc, h, d, w_gate, b_gate, gates, grad_o
         group = ctx.enter_context(tc.tile_pool(name="group", bufs=3))
         tcode = ctx.enter_context(tc.tile_pool(name="tcode", bufs=8))
         fcode = ctx.enter_context(tc.tile_pool(name="fcode", bufs=4))
-        stage = ctx.enter_context(tc.tile_pool(name="stage", bufs=6))
-        psum = ctx.enter_context(tc.psum_pool(name="psum", bufs=4))
-        ctx.enter_context(tc.manual_schedule())
+        stage = ctx.enter_context(tc.tile_pool(name="stage", bufs=10))
+        psum = ctx.enter_context(tc.psum_pool(name="psum", bufs=3))
+        psum_e = ctx.enter_context(tc.psum_pool(name="psum_e", bufs=2))
 
         minus_one = const.tile([P, 1], F32, name="minus_one")
         nc.vector.memset(minus_one[:], -1.0)
@@ -52,13 +52,16 @@ def tile_blockrecurrentmodel_pb_v_kernel(tc, h, d, w_gate, b_gate, gates, grad_o
         ident = const.tile([P, P], F32, name="ident")
         make_identity(nc, ident[:])
 
+        minus_ident = const.tile([P, P], BF16, name="minus_ident")
+        nc.vector.tensor_scalar(out=minus_ident[:], in0=ident[:], scalar1=-1.0, scalar2=None, op0=ALU.mult)
+
         w_codes = const.tile([P, BLOCKS, 3, BH], U32, name="w_codes", align_bytes=64)
         w_scales = const.tile([P, BLOCKS, 3, BH], U8, name="w_scales", align_bytes=64)
         h_codes = const.tile([P, 2, FEATURES], U32, name="h_codes", align_bytes=64)
         h_scales = const.tile([P, 2, FEATURES], U8, name="h_scales", align_bytes=64)
 
         gate_in, g_in, d_in, w_in = {}, {}, {}, {}
-        cand_t, q_t, a_t, dz = {}, {}, {}, {}
+        cand_t, q_t, a_t, e_t, dz = {}, {}, {}, {}, {}
         tok, feat, grouped = {}, {}, {}
 
         def rows(t):
@@ -73,14 +76,12 @@ def tile_blockrecurrentmodel_pb_v_kernel(tc, h, d, w_gate, b_gate, gates, grad_o
             width = BH // pieces
             for q in range(pieces):
                 ws = slice(q * width, (q + 1) * width)
-                for s in (R, C):
+                cols = slice(g * BH + q * width, g * BH + (q + 1) * width)
+                for s in (R, C, U):
                     src = gates[rows(t), g, s * BH + q * width : s * BH + (q + 1) * width]
                     nc.sync.dma_start(out=gate_in[i, s][:, :, ws], in_=src.rearrange("(p j) w -> p j w", j=PACK))
-            src = gates[rows(t), g, U * BH : (U + 1) * BH]
-            nc.sync.dma_start(out=gate_in[i, U][:], in_=src.rearrange("(p j) w -> p j w", j=PACK))
-            cols = slice(g * BH, (g + 1) * BH)
-            nc.sync.dma_start(out=g_in[i][:], in_=grad_out[rows(t), cols].rearrange("(p j) w -> p j w", j=PACK))
-            nc.sync.dma_start(out=d_in[i][:], in_=d[rows(t), cols].rearrange("(p j) w -> p j w", j=PACK))
+                for dst, src in ((g_in[i], grad_out), (d_in[i], d)):
+                    nc.sync.dma_start(out=dst[:, :, ws], in_=src[rows(t), cols].rearrange("(p j) w -> p j w", j=PACK))
 
         def load_w(g):
             w_in[g] = work.tile([P, BH // P, GATES], BF16, name="w_in", align_bytes=64)
@@ -97,8 +98,8 @@ def tile_blockrecurrentmodel_pb_v_kernel(tc, h, d, w_gate, b_gate, gates, grad_o
             return a[:, :, x * HALF : (x + 1) * HALF]
 
         def sig(i):
-            for s, bias in ((R, 0.0), (U, minus_one[:])):
-                for x in (0, 1):
+            for x in (0, 1):
+                for s, bias in ((R, 0.0), (U, minus_one[:])):
                     v = half(gate_in[i, s], x)
                     nc.scalar.activation(v, v, ACT.Sigmoid, bias=bias)
 
@@ -128,9 +129,23 @@ def tile_blockrecurrentmodel_pb_v_kernel(tc, h, d, w_gate, b_gate, gates, grad_o
             m = half(gate_in[i, C], x)
             stt(m, half(gate_in[i, R], x), -1.0, ALU.add, m)
 
-        def v_e(i, x):
-            e = half(cand_t[i], x)
-            nc.vector.tensor_tensor(out=e, in0=e, in1=half(d_in[i], x), op=ALU.subtract)
+        def quarter(a, k):
+            return a[:, :, k * P : (k + 1) * P]
+
+        def e_bank(i, k):
+            bank = psum_e.tile([P, PACK, P], F32, name="e")
+            e_t[i, k] = bank
+            nc.tensor.matmul(bank[:], lhsT=minus_ident[:], rhs=quarter(d_in[i], k), start=True, stop=False)
+            nc.tensor.matmul(bank[:], lhsT=ident[:], rhs=quarter(cand_t[i], k), start=False, stop=True)
+
+        def v_du(i, k):
+            view = "p j (c i) -> p c j i"
+            nc.vector.tensor_tensor(
+                out=dz[i, U][:, k * P : (k + 1) * P, :].rearrange("p (c i) j -> p c j i", i=4),
+                in0=quarter(gate_in[i, U], k).rearrange(view, i=4),
+                in1=e_t[i, k][:].rearrange(view, i=4),
+                op=ALU.mult,
+            )
 
         def v_dp(i, x):
             q = half(q_t[i], x)
@@ -139,7 +154,6 @@ def tile_blockrecurrentmodel_pb_v_kernel(tc, h, d, w_gate, b_gate, gates, grad_o
         def v_dz(i, s, x):
             in0, in1 = {
                 R: (gate_in[i, C], q_t[i]),
-                U: (gate_in[i, U], cand_t[i]),
                 C: (q_t[i], gate_in[i, R]),
             }[s]
             view = "p j (c i) -> p c j i"
@@ -166,7 +180,7 @@ def tile_blockrecurrentmodel_pb_v_kernel(tc, h, d, w_gate, b_gate, gates, grad_o
                 out=codes[:].bitcast(E5M2), scales=scales[:], in_=dz[i, s][:].rearrange("p w j -> p (w j)")
             )
 
-        def turn(i, s):
+        def turn(i, s, on_vector=()):
             words = dz[i, s][:].rearrange("p w j -> p (w j)").bitcast(F32)
             grp = group.tile([P, 2, 2, P, PACK], BF16, name="feat_grp", align_bytes=64)
             grouped[i, s] = grp
@@ -175,7 +189,8 @@ def tile_blockrecurrentmodel_pb_v_kernel(tc, h, d, w_gate, b_gate, gates, grad_o
                 for t in range(PACK):
                     nc.tensor.transpose(xt[:, t, :], words[:, 2 * t + u : 2 * BH : 8], ident[:])
                 src = xt[:].rearrange("p t q -> p (t q)").bitcast(BF16)
-                nc.scalar.copy(out=grp[:, u], in_=src.rearrange("p (t q e) -> p e q t", t=PACK, e=2))
+                copy = nc.vector.tensor_copy if u in on_vector else nc.scalar.copy
+                copy(out=grp[:, u], in_=src.rearrange("p (t q e) -> p e q t", t=PACK, e=2))
 
         def quant_feat(i, s):
             codes = fcode.tile([P, K_PASS], U32, name="feat_codes", align_bytes=64)
@@ -209,10 +224,10 @@ def tile_blockrecurrentmodel_pb_v_kernel(tc, h, d, w_gate, b_gate, gates, grad_o
                 in_=grouped["w", g, s][:].rearrange("p b o u e -> p (b o u e)"),
             )
 
-        def group_h(g, t):
+        def group_h(g, t, on_vector=False):
             grp = group.tile([P, BH, PACK], BF16, name="wh_grp", align_bytes=64)
             grouped["h", g, t] = grp
-            nc.scalar.copy(
+            (nc.vector.tensor_copy if on_vector else nc.scalar.copy)(
                 out=grp[:].rearrange("p (c i) j -> p c j i", i=4),
                 in_=w_in["h", g, t][:].rearrange("p j (c i) -> p c j i", i=4),
             )
@@ -233,7 +248,7 @@ def tile_blockrecurrentmodel_pb_v_kernel(tc, h, d, w_gate, b_gate, gates, grad_o
                 nc.scalar.copy(out=res[:], in_=acc[:])
             nc.sync.dma_start(out=dst, in_=res[:])
 
-        def product_h(i, split):
+        def product_h(i, split=()):
             g, t = chunks[i]
             dst = out_0[rows(t), g * BH : (g + 1) * BH].rearrange("(p j) w -> p j w", j=PACK)
             for j in range(PACK):
@@ -249,9 +264,9 @@ def tile_blockrecurrentmodel_pb_v_kernel(tc, h, d, w_gate, b_gate, gates, grad_o
                         start=n == 0,
                         stop=n == 2,
                     )
-                drain(acc, dst[:, j, :], split and j % 2 == 0)
+                drain(acc, dst[:, j, :], j in split)
 
-        def product_w(g, s, split):
+        def product_w(g, s, split=()):
             for m in range(BH // P):
                 acc = psum.tile([P, BH], F32, name="acc")
                 cols = slice(g * BH + m * P, g * BH + (m + 1) * P)
@@ -266,7 +281,7 @@ def tile_blockrecurrentmodel_pb_v_kernel(tc, h, d, w_gate, b_gate, gates, grad_o
                         start=t == 0,
                         stop=t == 1,
                     )
-                drain(acc, out_1[g, m * P : (m + 1) * P, s * BH : (s + 1) * BH], split and m % 2 == 0)
+                drain(acc, out_1[g, m * P : (m + 1) * P, s * BH : (s + 1) * BH], m in split)
 
         load_chunk(0, 2)
         load_w(0)
@@ -274,8 +289,9 @@ def tile_blockrecurrentmodel_pb_v_kernel(tc, h, d, w_gate, b_gate, gates, grad_o
         sig(0)
         for i in range(4):
             prev = i - 1
+            last = i == 3
             work_tiles(i)
-            if i + 1 < 4:
+            if not last:
                 load_chunk(i + 1, 1)
             if i == 0:
                 load_h(0, 1)
@@ -286,67 +302,72 @@ def tile_blockrecurrentmodel_pb_v_kernel(tc, h, d, w_gate, b_gate, gates, grad_o
                 load_h(1, 1)
 
             v_m(i, 0)
-            if prev >= 0:
-                quant_tok(prev, R)
             v_m(i, 1)
-            s_tanh(i)
-            s_square(i)
-            if prev >= 0:
-                quant_feat(prev, C)
+            with tc.high_priority(offset=100):
+                s_tanh(i)
+                for k in range(4):
+                    e_bank(i, k)
+                s_square(i)
+                if not last:
+                    sig(i + 1)
             v_a(i, 0)
             v_a(i, 1)
             v_b(i, 0)
-            if prev >= 0:
-                quant_feat(prev, R)
             v_b(i, 1)
-            if prev >= 0:
-                product_h(prev, False)
-            if i == 0:
-                for s in range(3):
-                    turn_w(0, s)
-            v_e(i, 0)
-            v_e(i, 1)
-            v_dz(i, U, 0)
-            v_dz(i, U, 1)
-            turn(i, U)
-            if i + 1 < 4:
-                sig(i + 1)
-            if i == 0:
-                group_h(0, 0)
-            elif i == 1:
-                group_h(0, 1)
-                for s in range(3):
-                    turn_w(1, s)
-            elif i == 2:
-                group_h(1, 0)
-                for s in range(3):
-                    product_w(0, s, False)
-            else:
-                group_h(1, 1)
+            for k in range(4):
+                v_du(i, k)
+            if last:
+                quant_feat(prev, R)
+                product_h(prev)
+                turn(i, U)
+                quant_tok(i, U)
             v_w(i, 0)
-            quant_tok(i, U)
             v_w(i, 1)
-            if i == 0:
-                for s in range(3):
-                    quant_w(0, s)
             v_dp(i, 0)
+            if last:
+                product_w(1, U)
+                quant_feat(i, U)
             v_dp(i, 1)
-            v_dz(i, C, 0)
-            quant_feat(i, U)
-            v_dz(i, C, 1)
-            turn(i, C)
-            if i == 1:
-                for s in range(3):
-                    quant_w(1, s)
-            v_dz(i, R, 0)
-            quant_tok(i, C)
-            quant_h(*((0, 0), (0, 1), (1, 0), (1, 1))[i])
-            v_dz(i, R, 1)
-            turn(i, R)
-        product_w(1, U, False)
-        quant_tok(3, R)
-        quant_feat(3, C)
-        product_w(1, C, True)
-        quant_feat(3, R)
-        product_w(1, R, True)
-        product_h(3, True)
+            for x in (0, 1):
+                v_dz(i, C, x)
+            if last:
+                turn(i, C, (1,))
+                quant_tok(i, C)
+                product_w(1, C, (0, 2))
+            for x in (0, 1):
+                v_dz(i, R, x)
+            if last:
+                turn(i, R, (1,))
+                quant_feat(i, C)
+                quant_tok(i, R)
+                product_w(1, R, (0, 2))
+                quant_feat(i, R)
+                product_h(i, (0, 2))
+            else:
+                if prev >= 0:
+                    quant_feat(prev, R)
+                    product_h(prev)
+                if i == 0:
+                    for s in range(3):
+                        turn_w(0, s)
+                        quant_w(0, s)
+                    group_h(0, 0)
+                    quant_h(0, 0)
+                elif i == 1:
+                    group_h(0, 1)
+                    quant_h(0, 1)
+                    for s in range(3):
+                        turn_w(1, s)
+                        quant_w(1, s)
+                    group_h(1, 0)
+                    quant_h(1, 0)
+                elif i == 2:
+                    group_h(1, 1)
+                    quant_h(1, 1)
+                    for s in range(3):
+                        product_w(0, s)
+                for s in (U, C, R):
+                    turn(i, s)
+                    quant_tok(i, s)
+                    if s != R:
+                        quant_feat(i, s)

@@ -44,6 +44,7 @@ def tile_blockrecurrentmodel_pb_v_kernel(tc, h, d, w_gate, b_gate, gates, grad_o
         stage = ctx.enter_context(tc.tile_pool(name="stage", bufs=10))
         psum = ctx.enter_context(tc.psum_pool(name="psum", bufs=3))
         psum_e = ctx.enter_context(tc.psum_pool(name="psum_e", bufs=2))
+        ctx.enter_context(tc.manual_schedule())
 
         minus_one = const.tile([P, 1], F32, name="minus_one")
         nc.vector.memset(minus_one[:], -1.0)
@@ -51,7 +52,6 @@ def tile_blockrecurrentmodel_pb_v_kernel(tc, h, d, w_gate, b_gate, gates, grad_o
         nc.scalar.activation(warm[:], minus_one[:], ACT.Sigmoid)
         ident = const.tile([P, P], F32, name="ident")
         make_identity(nc, ident[:])
-
         minus_ident = const.tile([P, P], BF16, name="minus_ident")
         nc.vector.tensor_scalar(out=minus_ident[:], in0=ident[:], scalar1=-1.0, scalar2=None, op0=ALU.mult)
 
@@ -60,176 +60,169 @@ def tile_blockrecurrentmodel_pb_v_kernel(tc, h, d, w_gate, b_gate, gates, grad_o
         h_codes = const.tile([P, 2, FEATURES], U32, name="h_codes", align_bytes=64)
         h_scales = const.tile([P, 2, FEATURES], U8, name="h_scales", align_bytes=64)
 
-        gate_in, g_in, d_in, w_in = {}, {}, {}, {}
-        cand_t, q_t, a_t, e_t, dz = {}, {}, {}, {}, {}
-        tok, feat, grouped = {}, {}, {}
+        T = {}
 
         def rows(t):
             return slice(K_PASS * t, K_PASS * (t + 1))
 
-        def load_chunk(i, pieces):
+        def n_of(i):
+            return PACK if i == 0 else 2
+
+        def part(a, x, n):
+            return a[:, x * PACK // n : (x + 1) * PACK // n, :]
+
+        def fresh(pool, name, key, dtype):
+            if key not in T:
+                T[key] = pool.tile([P, PACK, BH], dtype, name=name)
+            return T[key]
+
+        def load(i, what, x=0, n=1):
             g, t = chunks[i]
-            for s, nm in ((R, "r_in"), (C, "c_in"), (U, "u_in")):
-                gate_in[i, s] = stream.tile([P, PACK, BH], F32, name=nm)
-            g_in[i] = stream.tile([P, PACK, BH], BF16, name="g_in")
-            d_in[i] = stream.tile([P, PACK, BH], BF16, name="d_in")
-            width = BH // pieces
-            for q in range(pieces):
-                ws = slice(q * width, (q + 1) * width)
-                cols = slice(g * BH + q * width, g * BH + (q + 1) * width)
-                for s in (R, C, U):
-                    src = gates[rows(t), g, s * BH + q * width : s * BH + (q + 1) * width]
-                    nc.sync.dma_start(out=gate_in[i, s][:, :, ws], in_=src.rearrange("(p j) w -> p j w", j=PACK))
-                for dst, src in ((g_in[i], grad_out), (d_in[i], d)):
-                    nc.sync.dma_start(out=dst[:, :, ws], in_=src[rows(t), cols].rearrange("(p j) w -> p j w", j=PACK))
+            cols = slice(g * BH, (g + 1) * BH)
+            src = {
+                "r": gates[rows(t), g, 0:BH],
+                "u": gates[rows(t), g, BH : 2 * BH],
+                "c": gates[rows(t), g, 2 * BH : 3 * BH],
+                "g": grad_out[rows(t), cols],
+                "d": d[rows(t), cols],
+            }[what].rearrange("(p j) w -> p j w", j=PACK)
+            dst = fresh(stream, what + "_in", (what, i), F32 if what in "ruc" else BF16)
+            nc.sync.dma_start(out=part(dst, x, n), in_=part(src, x, n))
 
         def load_w(g):
-            w_in[g] = work.tile([P, BH // P, GATES], BF16, name="w_in", align_bytes=64)
-            nc.sync.dma_start(out=w_in[g][:], in_=w_gate[g].rearrange("(b p) k -> p b k", p=P))
+            T["w", g] = work.tile([P, BH // P, GATES], BF16, name="w_in", align_bytes=64)
+            nc.sync.dma_start(out=T["w", g][:], in_=w_gate[g].rearrange("(b p) k -> p b k", p=P))
 
         def load_h(g, t):
-            raw = stream.tile([P, PACK, BH], BF16, name="h_in")
-            w_in["h", g, t] = raw
-            nc.sync.dma_start(
-                out=raw[:], in_=h[rows(t), g * BH : (g + 1) * BH].rearrange("(p j) w -> p j w", j=PACK)
-            )
+            T["h", g, t] = stream.tile([P, PACK, BH], BF16, name="h_in")
+            src = h[rows(t), g * BH : (g + 1) * BH].rearrange("(p j) w -> p j w", j=PACK)
+            nc.sync.dma_start(out=T["h", g, t][:], in_=src)
 
-        def half(a, x):
-            return a[:, :, x * HALF : (x + 1) * HALF]
+        def sig(i, what, x):
+            v = part(T[what, i], x, n_of(i))
+            nc.scalar.activation(v, v, ACT.Sigmoid, bias=minus_one[:] if what == "u" else 0.0)
 
-        def sig(i):
-            for x in (0, 1):
-                for s, bias in ((R, 0.0), (U, minus_one[:])):
-                    v = half(gate_in[i, s], x)
-                    nc.scalar.activation(v, v, ACT.Sigmoid, bias=bias)
+        def tanh(i, x):
+            cand = fresh(work, "cand", ("cand", i), F32)
+            nc.scalar.activation(part(cand, x, n_of(i)), part(T["c", i], x, n_of(i)), ACT.Tanh, scale=-1.0)
 
-        def work_tiles(i):
-            cand_t[i] = work.tile([P, PACK, BH], F32, name="cand")
-            q_t[i] = work.tile([P, PACK, BH], F32, name="q")
-            a_t[i] = work.tile([P, PACK, BH], F32, name="a")
-            dz[i, R] = work.tile([P, BH, PACK], BF16, name="dr", align_bytes=64)
-            dz[i, U] = work.tile([P, BH, PACK], BF16, name="du", align_bytes=64)
-            dz[i, C] = work.tile([P, BH, PACK], BF16, name="dc", align_bytes=64)
+        def square(i, x):
+            q = fresh(work, "q", ("q", i), F32)
+            nc.scalar.activation(part(q, x, 2), part(T["cand", i], x, 2), ACT.Square)
 
         def stt(out, in0, scalar, op0, in1):
             nc.vector.scalar_tensor_tensor(out=out, in0=in0, scalar=scalar, in1=in1, op0=op0, op1=ALU.mult)
 
         def v_m(i, x):
-            c = half(gate_in[i, C], x)
-            stt(c, half(gate_in[i, R], x), -1.0, ALU.mult, c)
+            c = part(T["c", i], x, n_of(i))
+            stt(c, part(T["r", i], x, n_of(i)), -1.0, ALU.mult, c)
 
         def v_a(i, x):
-            stt(half(a_t[i], x), half(g_in[i], x), -1.0, ALU.mult, half(gate_in[i, U], x))
+            a = fresh(work, "a", ("a", i), F32)
+            stt(part(a, x, n_of(i)), part(T["g", i], x, n_of(i)), -1.0, ALU.mult, part(T["u", i], x, n_of(i)))
 
         def v_b(i, x):
-            u = half(gate_in[i, U], x)
-            stt(u, u, -1.0, ALU.add, half(a_t[i], x))
+            u = part(T["u", i], x, n_of(i))
+            stt(u, u, -1.0, ALU.add, part(T["a", i], x, n_of(i)))
 
         def v_w(i, x):
-            m = half(gate_in[i, C], x)
-            stt(m, half(gate_in[i, R], x), -1.0, ALU.add, m)
-
-        def quarter(a, k):
-            return a[:, :, k * P : (k + 1) * P]
-
-        def e_bank(i, k):
-            bank = psum_e.tile([P, PACK, P], F32, name="e")
-            e_t[i, k] = bank
-            nc.tensor.matmul(bank[:], lhsT=minus_ident[:], rhs=quarter(d_in[i], k), start=True, stop=False)
-            nc.tensor.matmul(bank[:], lhsT=ident[:], rhs=quarter(cand_t[i], k), start=False, stop=True)
-
-        def v_du(i, k):
-            view = "p j (c i) -> p c j i"
-            nc.vector.tensor_tensor(
-                out=dz[i, U][:, k * P : (k + 1) * P, :].rearrange("p (c i) j -> p c j i", i=4),
-                in0=quarter(gate_in[i, U], k).rearrange(view, i=4),
-                in1=e_t[i, k][:].rearrange(view, i=4),
-                op=ALU.mult,
-            )
+            m = part(T["c", i], x, n_of(i))
+            stt(m, part(T["r", i], x, n_of(i)), -1.0, ALU.add, m)
 
         def v_dp(i, x):
-            q = half(q_t[i], x)
-            stt(q, q, -1.0, ALU.add, half(a_t[i], x))
+            q = part(T["q", i], x, 2)
+            stt(q, q, -1.0, ALU.add, part(T["a", i], x, 2))
 
-        def v_dz(i, s, x):
-            in0, in1 = {
-                R: (gate_in[i, C], q_t[i]),
-                C: (q_t[i], gate_in[i, R]),
-            }[s]
+        def e_bank(i, k):
+            cols = slice(k * P, (k + 1) * P)
+            bank = psum_e.tile([P, PACK, P], F32, name="e")
+            T["e", i, k] = bank
+            nc.tensor.matmul(bank[:], lhsT=minus_ident[:], rhs=T["d", i][:, :, cols], start=True, stop=False)
+            nc.tensor.matmul(bank[:], lhsT=ident[:], rhs=T["cand", i][:, :, cols], start=False, stop=True)
+
+        def gradient(i, s, lo, hi, in0, in1):
+            if ("dz", i, s) not in T:
+                T["dz", i, s] = work.tile([P, BH, PACK], BF16, name="dz" + "ruc"[s], align_bytes=64)
             view = "p j (c i) -> p c j i"
             nc.vector.tensor_tensor(
-                out=dz[i, s][:, x * HALF : (x + 1) * HALF, :].rearrange("p (c i) j -> p c j i", i=4),
-                in0=half(in0, x).rearrange(view, i=4),
-                in1=half(in1, x).rearrange(view, i=4),
+                out=T["dz", i, s][:, lo:hi, :].rearrange("p (c i) j -> p c j i", i=4),
+                in0=in0[:, :, lo:hi].rearrange(view, i=4),
+                in1=in1.rearrange(view, i=4),
                 op=ALU.mult,
             )
 
-        def s_tanh(i):
-            for x in (0, 1):
-                nc.scalar.activation(half(cand_t[i], x), half(gate_in[i, C], x), ACT.Tanh, scale=-1.0)
+        def v_du(i, k):
+            gradient(i, U, k * P, (k + 1) * P, T["u", i], T["e", i, k][:])
 
-        def s_square(i):
-            for x in (0, 1):
-                nc.scalar.activation(half(q_t[i], x), half(cand_t[i], x), ACT.Square)
+        def v_dc(i, x):
+            gradient(i, C, x * HALF, (x + 1) * HALF, T["q", i], T["r", i][:, :, x * HALF : (x + 1) * HALF])
+
+        def v_dr(i, x):
+            gradient(i, R, x * HALF, (x + 1) * HALF, T["c", i], T["q", i][:, :, x * HALF : (x + 1) * HALF])
 
         def quant_tok(i, s):
             codes = tcode.tile([P, BH], U32, name="tok_codes", align_bytes=64)
             scales = tcode.tile([P, BH], U8, name="tok_scales", align_bytes=64)
-            tok[i, s] = (codes, scales)
+            T["tok", i, s] = (codes, scales)
             nc.vector.quantize_mx(
-                out=codes[:].bitcast(E5M2), scales=scales[:], in_=dz[i, s][:].rearrange("p w j -> p (w j)")
+                out=codes[:].bitcast(E5M2), scales=scales[:], in_=T["dz", i, s][:].rearrange("p w j -> p (w j)")
             )
 
-        def turn(i, s, on_vector=()):
-            words = dz[i, s][:].rearrange("p w j -> p (w j)").bitcast(F32)
-            grp = group.tile([P, 2, 2, P, PACK], BF16, name="feat_grp", align_bytes=64)
-            grouped[i, s] = grp
-            for u in (0, 1):
-                xt = psum.tile([P, PACK, P], F32, name="xt")
-                for t in range(PACK):
-                    nc.tensor.transpose(xt[:, t, :], words[:, 2 * t + u : 2 * BH : 8], ident[:])
-                src = xt[:].rearrange("p t q -> p (t q)").bitcast(BF16)
-                copy = nc.vector.tensor_copy if u in on_vector else nc.scalar.copy
-                copy(out=grp[:, u], in_=src.rearrange("p (t q e) -> p e q t", t=PACK, e=2))
+        def turn(i, s, u):
+            words = T["dz", i, s][:].rearrange("p w j -> p (w j)").bitcast(F32)
+            bank = psum.tile([P, PACK, P], F32, name="xt")
+            T["xt", i, s, u] = bank
+            for t in range(PACK):
+                nc.tensor.transpose(bank[:, t, :], words[:, 2 * t + u : 2 * BH : 8], ident[:])
+
+        def regroup(i, s, u, on_vector=False):
+            if ("fg", i, s) not in T:
+                T["fg", i, s] = group.tile([P, 2, 2, P, PACK], BF16, name="feat_grp", align_bytes=64)
+            src = T["xt", i, s, u][:].rearrange("p t q -> p (t q)").bitcast(BF16)
+            copy = nc.vector.tensor_copy if on_vector else nc.scalar.copy
+            copy(out=T["fg", i, s][:, u], in_=src.rearrange("p (t q e) -> p e q t", t=PACK, e=2))
 
         def quant_feat(i, s):
             codes = fcode.tile([P, K_PASS], U32, name="feat_codes", align_bytes=64)
             scales = fcode.tile([P, K_PASS], U8, name="feat_scales", align_bytes=64)
-            feat[i, s] = (codes, scales)
+            T["feat", i, s] = (codes, scales)
             nc.vector.quantize_mx(
                 out=codes[:].bitcast(E5M2),
                 scales=scales[:],
-                in_=grouped[i, s][:].rearrange("p u e q t -> p (u e q t)"),
+                in_=T["fg", i, s][:].rearrange("p u e q t -> p (u e q t)"),
             )
 
-        def turn_w(g, s):
-            grp = group.tile([P, BH // P, P, 2, 2], BF16, name="wh_grp", align_bytes=64)
-            grouped["w", g, s] = grp
-            words = [w_in[g][:, b, :].bitcast(F32) for b in range(BH // P)]
-            dst = grp[:].rearrange("p b o u e -> p (b o u e)").bitcast(F32)
-            for b2 in (0, 1):
-                xt = psum.tile([P, PACK, P], F32, name="xt")
-                for k in range(4):
-                    b, u = 2 * b2 + k // 2, k % 2
-                    nc.tensor.transpose(xt[:, k, :], words[b][:, 256 * s + u : 256 * (s + 1) : 2], ident[:])
-                nc.scalar.copy(
-                    out=dst[:, 512 * b2 : 512 * (b2 + 1)].rearrange("p (b o u) -> p b o u", b=2, u=2),
-                    in_=xt[:].rearrange("p (b u) o -> p b o u", u=2),
-                )
+        def turn_w(g, s, b2):
+            bank = psum.tile([P, PACK, P], F32, name="xt")
+            T["xw", g, s, b2] = bank
+            for k in range(4):
+                words = T["w", g][:, 2 * b2 + k // 2, :].bitcast(F32)
+                nc.tensor.transpose(bank[:, k, :], words[:, 256 * s + k % 2 : 256 * (s + 1) : 2], ident[:])
+
+        def regroup_w(g, s, b2):
+            if ("wg", g, s) not in T:
+                T["wg", g, s] = group.tile([P, BH // P, P, 2, 2], BF16, name="wh_grp", align_bytes=64)
+            dst = T["wg", g, s][:].rearrange("p b o u e -> p (b o u e)").bitcast(F32)
+            nc.scalar.copy(
+                out=dst[:, 512 * b2 : 512 * (b2 + 1)].rearrange("p (b o u) -> p b o u", b=2, u=2),
+                in_=T["xw", g, s, b2][:].rearrange("p (b u) o -> p b o u", u=2),
+            )
 
         def quant_w(g, s):
             nc.vector.quantize_mx(
                 out=w_codes[:, g, s, :].bitcast(E4M3),
                 scales=w_scales[:, g, s, :],
-                in_=grouped["w", g, s][:].rearrange("p b o u e -> p (b o u e)"),
+                in_=T["wg", g, s][:].rearrange("p b o u e -> p (b o u e)"),
             )
 
-        def group_h(g, t, on_vector=False):
-            grp = group.tile([P, BH, PACK], BF16, name="wh_grp", align_bytes=64)
-            grouped["h", g, t] = grp
-            (nc.vector.tensor_copy if on_vector else nc.scalar.copy)(
-                out=grp[:].rearrange("p (c i) j -> p c j i", i=4),
-                in_=w_in["h", g, t][:].rearrange("p j (c i) -> p c j i", i=4),
+        def group_h(g, t, x, on_vector=False):
+            if ("hg", g, t) not in T:
+                T["hg", g, t] = group.tile([P, BH, PACK], BF16, name="wh_grp", align_bytes=64)
+            ws = slice(x * HALF, (x + 1) * HALF)
+            copy = nc.vector.tensor_copy if on_vector else nc.scalar.copy
+            copy(
+                out=T["hg", g, t][:, ws, :].rearrange("p (c i) j -> p c j i", i=4),
+                in_=T["h", g, t][:, :, ws].rearrange("p j (c i) -> p c j i", i=4),
             )
 
         def quant_h(g, t):
@@ -237,7 +230,7 @@ def tile_blockrecurrentmodel_pb_v_kernel(tc, h, d, w_gate, b_gate, gates, grad_o
             nc.vector.quantize_mx(
                 out=h_codes[:, t, cols].bitcast(E4M3),
                 scales=h_scales[:, t, cols],
-                in_=grouped["h", g, t][:].rearrange("p w j -> p (w j)"),
+                in_=T["hg", g, t][:].rearrange("p w j -> p (w j)"),
             )
 
         def drain(acc, dst, on_vector):
@@ -248,126 +241,432 @@ def tile_blockrecurrentmodel_pb_v_kernel(tc, h, d, w_gate, b_gate, gates, grad_o
                 nc.scalar.copy(out=res[:], in_=acc[:])
             nc.sync.dma_start(out=dst, in_=res[:])
 
-        def product_h(i, split=()):
+        def open_h(i, j, where):
+            if where == "e":
+                acc = psum_e.tile([P, BH], F32, name="e")
+            elif where == "xt":
+                acc = psum.tile([P, BH], F32, name="xt")
+            else:
+                acc = psum.tile([P, BH], F32, name="acc")
+            T["acc", i, j] = acc
+
+        def pass_h(i, j, s, start, stop):
+            codes, scales = T["feat", i, s]
+            g = chunks[i][0]
+            nc.tensor.matmul_mx(
+                out=T["acc", i, j][:],
+                lhsT=codes[:, j * P : (j + 1) * P].bitcast(E5M2),
+                lhsT_scale=scales[:, j * P : (j + 1) * P],
+                rhs=w_codes[:, g, s, :].bitcast(E4M3),
+                rhs_scale=w_scales[:, g, s, :],
+                start=start,
+                stop=stop,
+            )
+
+        def drain_h(i, j, on_vector=False):
             g, t = chunks[i]
             dst = out_0[rows(t), g * BH : (g + 1) * BH].rearrange("(p j) w -> p j w", j=PACK)
-            for j in range(PACK):
-                acc = psum.tile([P, BH], F32, name="acc")
-                for n, s in enumerate((U, C, R)):
-                    codes, scales = feat[i, s]
-                    nc.tensor.matmul_mx(
-                        out=acc[:],
-                        lhsT=codes[:, j * P : (j + 1) * P].bitcast(E5M2),
-                        lhsT_scale=scales[:, j * P : (j + 1) * P],
-                        rhs=w_codes[:, g, s, :].bitcast(E4M3),
-                        rhs_scale=w_scales[:, g, s, :],
-                        start=n == 0,
-                        stop=n == 2,
-                    )
-                drain(acc, dst[:, j, :], j in split)
+            drain(T["acc", i, j], dst[:, j, :], on_vector)
 
-        def product_w(g, s, split=()):
-            for m in range(BH // P):
-                acc = psum.tile([P, BH], F32, name="acc")
-                cols = slice(g * BH + m * P, g * BH + (m + 1) * P)
-                for t in (0, 1):
-                    codes, scales = tok[2 * g + t, s]
-                    nc.tensor.matmul_mx(
-                        out=acc[:],
-                        lhsT=h_codes[:, t, cols].bitcast(E4M3),
-                        lhsT_scale=h_scales[:, t, cols],
-                        rhs=codes[:].bitcast(E5M2),
-                        rhs_scale=scales[:],
-                        start=t == 0,
-                        stop=t == 1,
-                    )
-                drain(acc, out_1[g, m * P : (m + 1) * P, s * BH : (s + 1) * BH], m in split)
+        def product_h(i, j):
+            open_h(i, j, "acc")
+            for s in (U, C, R):
+                pass_h(i, j, s, s == U, s == R)
 
-        load_chunk(0, 2)
+        def begin_h(i, j):
+            open_h(i, j, "e" if j < 2 else "xt")
+            pass_h(i, j, U, True, False)
+            pass_h(i, j, C, False, False)
+
+        def end_h(i, j):
+            pass_h(i, j, R, False, True)
+
+        def product_w(g, s, m):
+            acc = psum.tile([P, BH], F32, name="acc")
+            T["accw", g, s, m] = acc
+            cols = slice(g * BH + m * P, g * BH + (m + 1) * P)
+            for t in (0, 1):
+                codes, scales = T["tok", 2 * g + t, s]
+                nc.tensor.matmul_mx(
+                    out=acc[:],
+                    lhsT=h_codes[:, t, cols].bitcast(E4M3),
+                    lhsT_scale=h_scales[:, t, cols],
+                    rhs=codes[:].bitcast(E5M2),
+                    rhs_scale=scales[:],
+                    start=t == 0,
+                    stop=t == 1,
+                )
+
+        def drain_w(g, s, m, on_vector=False):
+            drain(T["accw", g, s, m], out_1[g, m * P : (m + 1) * P, s * BH : (s + 1) * BH], on_vector)
+
+        load(0, "r", 3, 4)
+        load(0, "c", 3, 4)
+        sig(0, "r", 3)
+        v_m(0, 3)
+        tanh(0, 3)
+        load_h(0, 1)
+        group_h(0, 1, 1, True)
+        group_h(0, 1, 0, True)
+        load(0, "r", 2, 4)
+        quant_h(0, 1)
+        load(0, "u", 0, 4)
+        sig(0, "u", 0)
+        sig(0, "r", 2)
+        load(0, "g", 0, 4)
+        v_a(0, 0)
+        load(0, "u", 1, 4)
+        sig(0, "u", 1)
+        load(0, "c", 2, 4)
+        v_m(0, 2)
+        v_b(0, 0)
+        load(0, "g", 1, 4)
+        v_w(0, 3)
+        load(0, "u", 3, 4)
+        sig(0, "u", 3)
+        v_a(0, 1)
+        load(0, "u", 2, 4)
+        load(0, "g", 2, 4)
+        sig(0, "u", 2)
+        v_a(0, 2)
+        load(0, "r", 0, 4)
+        sig(0, "r", 0)
+        load(0, "r", 1, 4)
+        load(0, "g", 3, 4)
+        v_b(0, 1)
+        v_a(0, 3)
+        tanh(0, 2)
+        sig(0, "r", 1)
+        load(0, "c", 0, 4)
+        v_m(0, 0)
+        tanh(0, 0)
+        load(0, "c", 1, 4)
+        v_m(0, 1)
+        v_w(0, 2)
+        load(0, "d")
         load_w(0)
         load_h(0, 0)
-        sig(0)
-        for i in range(4):
-            prev = i - 1
-            last = i == 3
-            work_tiles(i)
-            if not last:
-                load_chunk(i + 1, 1)
-            if i == 0:
-                load_h(0, 1)
-            elif i == 1:
-                load_w(1)
-                load_h(1, 0)
-            elif i == 2:
-                load_h(1, 1)
-
-            v_m(i, 0)
-            v_m(i, 1)
-            with tc.high_priority(offset=100):
-                s_tanh(i)
-                for k in range(4):
-                    e_bank(i, k)
-                s_square(i)
-                if not last:
-                    sig(i + 1)
-            v_a(i, 0)
-            v_a(i, 1)
-            v_b(i, 0)
-            v_b(i, 1)
-            for k in range(4):
-                v_du(i, k)
-            if last:
-                quant_feat(prev, R)
-                product_h(prev)
-                turn(i, U)
-                quant_tok(i, U)
-            v_w(i, 0)
-            v_w(i, 1)
-            v_dp(i, 0)
-            if last:
-                product_w(1, U)
-                quant_feat(i, U)
-            v_dp(i, 1)
-            for x in (0, 1):
-                v_dz(i, C, x)
-            if last:
-                turn(i, C, (1,))
-                quant_tok(i, C)
-                product_w(1, C, (0, 2))
-            for x in (0, 1):
-                v_dz(i, R, x)
-            if last:
-                turn(i, R, (1,))
-                quant_feat(i, C)
-                quant_tok(i, R)
-                product_w(1, R, (0, 2))
-                quant_feat(i, R)
-                product_h(i, (0, 2))
-            else:
-                if prev >= 0:
-                    quant_feat(prev, R)
-                    product_h(prev)
-                if i == 0:
-                    for s in range(3):
-                        turn_w(0, s)
-                        quant_w(0, s)
-                    group_h(0, 0)
-                    quant_h(0, 0)
-                elif i == 1:
-                    group_h(0, 1)
-                    quant_h(0, 1)
-                    for s in range(3):
-                        turn_w(1, s)
-                        quant_w(1, s)
-                    group_h(1, 0)
-                    quant_h(1, 0)
-                elif i == 2:
-                    group_h(1, 1)
-                    quant_h(1, 1)
-                    for s in range(3):
-                        product_w(0, s)
-                for s in (U, C, R):
-                    turn(i, s)
-                    quant_tok(i, s)
-                    if s != R:
-                        quant_feat(i, s)
+        tanh(0, 1)
+        v_w(0, 0)
+        square(0, 1)
+        e_bank(0, 1)
+        v_b(0, 3)
+        square(0, 0)
+        turn_w(0, 2, 1)
+        regroup_w(0, 2, 1)
+        turn_w(0, 2, 0)
+        regroup_w(0, 2, 0)
+        turn_w(0, 1, 1)
+        v_b(0, 2)
+        v_dp(0, 1)
+        group_h(0, 0, 1)
+        regroup_w(0, 1, 1)
+        v_dp(0, 0)
+        v_w(0, 1)
+        v_dc(0, 0)
+        v_dc(0, 1)
+        load(1, "r")
+        load(1, "c")
+        sig(1, "r", 0)
+        e_bank(0, 2)
+        v_dr(0, 1)
+        quant_w(0, 2)
+        load(1, "u")
+        load(1, "g")
+        turn_w(0, 0, 0)
+        v_du(0, 1)
+        sig(1, "r", 1)
+        v_du(0, 2)
+        turn_w(0, 1, 0)
+        e_bank(0, 3)
+        v_dr(0, 0)
+        turn(0, 0, 0)
+        quant_tok(0, 2)
+        group_h(0, 0, 0)
+        v_du(0, 3)
+        regroup_w(0, 0, 0)
+        v_m(1, 0)
+        quant_tok(0, 0)
+        turn(0, 2, 0)
+        regroup_w(0, 1, 0)
+        v_m(1, 1)
+        load_h(1, 1)
+        sig(1, "u", 0)
+        v_a(1, 0)
+        turn_w(0, 0, 1)
+        sig(1, "u", 1)
+        e_bank(0, 0)
+        load(1, "d")
+        v_du(0, 0)
+        regroup(0, 2, 0)
+        regroup_w(0, 0, 1)
+        quant_w(0, 1)
+        v_a(1, 1)
+        quant_w(0, 0)
+        load_w(1)
+        regroup(0, 0, 0)
+        turn(0, 2, 1)
+        tanh(1, 0)
+        quant_tok(0, 1)
+        quant_h(0, 0)
+        regroup(0, 2, 1)
+        v_b(1, 0)
+        turn(0, 0, 1)
+        turn(0, 1, 0)
+        tanh(1, 1)
+        square(1, 0)
+        v_b(1, 1)
+        turn(0, 1, 1)
+        v_dp(1, 0)
+        regroup(0, 1, 1)
+        square(1, 1)
+        load_h(1, 0)
+        load(2, "d")
+        e_bank(1, 1)
+        regroup(0, 0, 1)
+        e_bank(1, 2)
+        v_du(1, 1)
+        v_w(1, 0)
+        v_du(1, 2)
+        quant_feat(0, 2)
+        v_dp(1, 1)
+        regroup(0, 1, 0)
+        group_h(1, 0, 1)
+        e_bank(1, 0)
+        load(2, "g")
+        quant_feat(0, 1)
+        quant_feat(0, 0)
+        v_w(1, 1)
+        v_dc(1, 0)
+        turn_w(1, 1, 1)
+        turn_w(1, 1, 0)
+        regroup_w(1, 1, 0)
+        load(2, "u")
+        regroup_w(1, 1, 1)
+        e_bank(1, 3)
+        v_du(1, 3)
+        product_h(0, 1)
+        load(2, "r")
+        load(2, "c")
+        sig(2, "u", 1)
+        sig(2, "r", 1)
+        v_du(1, 0)
+        product_h(0, 3)
+        v_dc(1, 1)
+        group_h(1, 0, 0)
+        load(3, "r")
+        load(3, "u")
+        v_a(2, 1)
+        turn_w(1, 0, 1)
+        regroup_w(1, 0, 1)
+        quant_tok(1, 1)
+        sig(2, "r", 0)
+        v_m(2, 0)
+        product_h(0, 2)
+        sig(2, "u", 0)
+        drain_h(0, 2)
+        v_m(2, 1)
+        drain_h(0, 3)
+        v_dr(1, 0)
+        v_dr(1, 1)
+        turn(1, 1, 1)
+        drain_h(0, 1, True)
+        regroup(1, 1, 1)
+        tanh(2, 0)
+        v_w(2, 0)
+        load(3, "c")
+        turn_w(1, 0, 0)
+        tanh(2, 1)
+        square(2, 0)
+        v_b(2, 1)
+        turn(1, 0, 0)
+        regroup(1, 0, 0)
+        product_h(0, 0)
+        e_bank(2, 1)
+        quant_tok(1, 0)
+        regroup_w(1, 0, 0)
+        turn(1, 2, 0)
+        square(2, 1)
+        quant_tok(1, 2)
+        regroup(1, 2, 0)
+        quant_w(1, 0)
+        drain_h(0, 0)
+        product_w(0, 1, 3)
+        product_w(0, 2, 0)
+        turn(1, 2, 1)
+        drain_w(0, 1, 3)
+        e_bank(2, 3)
+        v_a(2, 0)
+        v_dp(2, 1)
+        turn(1, 1, 0)
+        sig(3, "r", 1)
+        product_w(0, 0, 0)
+        quant_w(1, 1)
+        v_b(2, 0)
+        quant_h(1, 0)
+        drain_w(0, 2, 0)
+        load(3, "g")
+        v_du(2, 1)
+        v_dp(2, 0)
+        load(3, "d")
+        turn(1, 0, 1)
+        regroup(1, 2, 1)
+        regroup(1, 1, 0)
+        turn_w(1, 2, 0)
+        drain_w(0, 0, 0)
+        e_bank(2, 2)
+        turn_w(1, 2, 1)
+        sig(3, "r", 0)
+        quant_feat(1, 2)
+        sig(3, "u", 0)
+        group_h(1, 1, 0)
+        regroup(1, 0, 1)
+        regroup_w(1, 2, 1)
+        v_dc(2, 1)
+        v_du(2, 3)
+        v_dc(2, 0)
+        quant_feat(1, 1)
+        e_bank(2, 0)
+        v_w(2, 1)
+        quant_feat(1, 0)
+        v_dr(2, 1)
+        product_w(0, 0, 3)
+        drain_w(0, 0, 3)
+        product_w(0, 1, 0)
+        v_dr(2, 0)
+        v_a(3, 0)
+        regroup_w(1, 2, 0)
+        product_h(1, 1)
+        v_du(2, 0)
+        v_m(3, 0)
+        sig(3, "u", 1)
+        product_h(1, 0)
+        drain_w(0, 1, 0)
+        drain_h(1, 0)
+        turn(2, 2, 1)
+        drain_h(1, 1)
+        turn(2, 0, 1)
+        v_du(2, 2)
+        product_w(0, 1, 1)
+        turn(2, 0, 0)
+        product_h(1, 2)
+        regroup(2, 2, 1)
+        regroup(2, 0, 1)
+        turn(2, 2, 0)
+        turn(2, 1, 1)
+        regroup(2, 0, 0)
+        product_h(1, 3)
+        v_m(3, 1)
+        tanh(3, 0)
+        drain_w(0, 1, 1)
+        tanh(3, 1)
+        drain_h(1, 3)
+        quant_tok(2, 1)
+        drain_h(1, 2)
+        square(3, 1)
+        turn(2, 1, 0)
+        product_w(0, 0, 2)
+        e_bank(3, 0)
+        regroup(2, 1, 1)
+        regroup(2, 1, 0)
+        regroup(2, 2, 0)
+        e_bank(3, 2)
+        v_a(3, 1)
+        v_b(3, 0)
+        v_b(3, 1)
+        drain_w(0, 0, 2)
+        v_w(3, 1)
+        v_du(3, 0)
+        quant_w(1, 2)
+        product_w(0, 2, 2)
+        drain_w(0, 2, 2)
+        v_du(3, 2)
+        product_w(0, 2, 3)
+        drain_w(0, 2, 3)
+        group_h(1, 1, 1, True)
+        e_bank(3, 3)
+        e_bank(3, 1)
+        product_w(0, 1, 2)
+        quant_feat(2, 0)
+        quant_feat(2, 1)
+        v_du(3, 3)
+        quant_feat(2, 2)
+        v_du(3, 1)
+        square(3, 0)
+        product_h(2, 1)
+        turn(3, 1, 1)
+        drain_w(0, 1, 2)
+        drain_h(2, 1)
+        quant_h(1, 1)
+        quant_tok(3, 1)
+        product_h(2, 0)
+        drain_h(2, 0)
+        product_w(0, 2, 1)
+        v_dp(3, 0)
+        drain_w(0, 2, 1)
+        product_w(1, 1, 2)
+        v_dp(3, 1)
+        quant_tok(2, 2)
+        drain_w(1, 1, 2)
+        product_w(0, 0, 1)
+        product_w(1, 1, 1)
+        drain_w(0, 0, 1)
+        product_w(1, 1, 0)
+        v_dc(3, 1)
+        product_h(2, 2)
+        drain_w(1, 1, 1)
+        regroup(3, 1, 1)
+        drain_h(2, 2)
+        drain_w(1, 1, 0)
+        product_h(2, 3)
+        v_dc(3, 0)
+        turn(3, 2, 1)
+        turn(3, 1, 0)
+        regroup(3, 2, 1)
+        turn(3, 2, 0)
+        v_w(3, 0)
+        quant_tok(3, 2)
+        drain_h(2, 3)
+        quant_tok(2, 0)
+        product_w(1, 2, 2)
+        drain_w(1, 2, 2)
+        v_dr(3, 0)
+        v_dr(3, 1)
+        product_w(1, 2, 0)
+        drain_w(1, 2, 0)
+        regroup(3, 2, 0)
+        regroup(3, 1, 0, True)
+        product_w(1, 1, 3)
+        drain_w(1, 1, 3)
+        product_w(1, 2, 1)
+        product_w(1, 2, 3)
+        turn(3, 0, 0)
+        turn(3, 0, 1)
+        quant_tok(3, 0)
+        quant_feat(3, 2)
+        quant_feat(3, 1)
+        drain_w(1, 2, 3)
+        drain_w(1, 2, 1)
+        regroup(3, 0, 0)
+        regroup(3, 0, 1, True)
+        product_w(1, 0, 1)
+        quant_feat(3, 0)
+        drain_w(1, 0, 1)
+        product_w(1, 0, 0)
+        drain_w(1, 0, 0)
+        begin_h(3, 0)
+        product_w(1, 0, 2)
+        drain_w(1, 0, 2, True)
+        begin_h(3, 3)
+        end_h(3, 0)
+        end_h(3, 3)
+        drain_h(3, 0)
+        product_w(1, 0, 3)
+        drain_h(3, 3)
+        begin_h(3, 2)
+        end_h(3, 2)
+        drain_w(1, 0, 3)
+        drain_h(3, 2)
+        begin_h(3, 1)
+        end_h(3, 1)
+        drain_h(3, 1)

from contextlib import ExitStack

import concourse.mybir as mybir
from concourse.masks import make_identity

TOKENS, FEATURES, BLOCKS = 1024, 1024, 2
BH = FEATURES // BLOCKS
GATES = 3 * BH

FLOPS = 2 * (2 * TOKENS * BLOCKS * BH * GATES)
BYTES = 2 * (3 * TOKENS * FEATURES + BLOCKS * BH * GATES) + 4 * (
    TOKENS * BLOCKS * GATES + TOKENS * FEATURES + BLOCKS * BH * GATES
)

F32 = mybir.dt.float32
BF16 = mybir.dt.bfloat16
U32 = mybir.dt.uint32
U8 = mybir.dt.uint8
E4M3 = mybir.dt.float8_e4m3fn_x4
E5M2 = mybir.dt.float8_e5m2_x4
ALU = mybir.AluOpType
ACT = mybir.ActivationFunctionType

P = 128
PACK = 4
K_PASS = P * PACK
HALF = BH // 2
R, U, C = 0, 1, 2


def tile_blockrecurrentmodel_pb_v_kernel(tc, h, d, w_gate, b_gate, gates, grad_out, out_0, out_1):
    nc = tc.nc
    d = d.flatten_outer_dims()
    grad_out = grad_out.flatten_outer_dims()
    chunks = [(g, t) for g in range(BLOCKS) for t in range(TOKENS // K_PASS)]

    with ExitStack() as ctx:
        const = ctx.enter_context(tc.tile_pool(name="const", bufs=1))
        stream = ctx.enter_context(tc.tile_pool(name="stream", bufs=2))
        work = ctx.enter_context(tc.tile_pool(name="work", bufs=1))
        group = ctx.enter_context(tc.tile_pool(name="group", bufs=3))
        tcode = ctx.enter_context(tc.tile_pool(name="tcode", bufs=8))
        fcode = ctx.enter_context(tc.tile_pool(name="fcode", bufs=4))
        stage = ctx.enter_context(tc.tile_pool(name="stage", bufs=10))
        psum = ctx.enter_context(tc.psum_pool(name="psum", bufs=3))
        psum_e = ctx.enter_context(tc.psum_pool(name="psum_e", bufs=2))
        ctx.enter_context(tc.manual_schedule())

        minus_one = const.tile([P, 1], F32, name="minus_one")
        nc.vector.memset(minus_one[:], -1.0)
        warm = const.tile([P, 1], F32, name="warm")
        nc.scalar.activation(warm[:], minus_one[:], ACT.Sigmoid)
        ident = const.tile([P, P], F32, name="ident")
        make_identity(nc, ident[:])
        minus_ident = const.tile([P, P], BF16, name="minus_ident")
        nc.vector.tensor_scalar(out=minus_ident[:], in0=ident[:], scalar1=-1.0, scalar2=None, op0=ALU.mult)

        w_codes = const.tile([P, BLOCKS, 3, BH], U32, name="w_codes", align_bytes=64)
        w_scales = const.tile([P, BLOCKS, 3, BH], U8, name="w_scales", align_bytes=64)
        h_codes = const.tile([P, 2, FEATURES], U32, name="h_codes", align_bytes=64)
        h_scales = const.tile([P, 2, FEATURES], U8, name="h_scales", align_bytes=64)

        T = {}

        def rows(t):
            return slice(K_PASS * t, K_PASS * (t + 1))

        def n_of(i):
            return PACK if i == 0 else 2

        def part(a, x, n):
            return a[:, x * PACK // n : (x + 1) * PACK // n, :]

        def fresh(pool, name, key, dtype):
            if key not in T:
                T[key] = pool.tile([P, PACK, BH], dtype, name=name)
            return T[key]

        def load(i, what, x=0, n=1):
            g, t = chunks[i]
            cols = slice(g * BH, (g + 1) * BH)
            src = {
                "r": gates[rows(t), g, 0:BH],
                "u": gates[rows(t), g, BH : 2 * BH],
                "c": gates[rows(t), g, 2 * BH : 3 * BH],
                "g": grad_out[rows(t), cols],
                "d": d[rows(t), cols],
            }[what].rearrange("(p j) w -> p j w", j=PACK)
            dst = fresh(stream, what + "_in", (what, i), F32 if what in "ruc" else BF16)
            nc.sync.dma_start(out=part(dst, x, n), in_=part(src, x, n))

        def load_w(g):
            T["w", g] = work.tile([P, BH // P, GATES], BF16, name="w_in", align_bytes=64)
            nc.sync.dma_start(out=T["w", g][:], in_=w_gate[g].rearrange("(b p) k -> p b k", p=P))

        def load_h(g, t):
            T["h", g, t] = stream.tile([P, PACK, BH], BF16, name="h_in")
            src = h[rows(t), g * BH : (g + 1) * BH].rearrange("(p j) w -> p j w", j=PACK)
            nc.sync.dma_start(out=T["h", g, t][:], in_=src)

        def sig(i, what, x):
            v = part(T[what, i], x, n_of(i))
            nc.scalar.activation(v, v, ACT.Sigmoid, bias=minus_one[:] if what == "u" else 0.0)

        def tanh(i, x):
            cand = fresh(work, "cand", ("cand", i), F32)
            nc.scalar.activation(part(cand, x, n_of(i)), part(T["c", i], x, n_of(i)), ACT.Tanh, scale=-1.0)

        def square(i, x):
            q = fresh(work, "q", ("q", i), F32)
            nc.scalar.activation(part(q, x, 2), part(T["cand", i], x, 2), ACT.Square)

        def stt(out, in0, scalar, op0, in1):
            nc.vector.scalar_tensor_tensor(out=out, in0=in0, scalar=scalar, in1=in1, op0=op0, op1=ALU.mult)

        def v_m(i, x):
            c = part(T["c", i], x, n_of(i))
            stt(c, part(T["r", i], x, n_of(i)), -1.0, ALU.mult, c)

        def v_a(i, x):
            a = fresh(work, "a", ("a", i), F32)
            stt(part(a, x, n_of(i)), part(T["g", i], x, n_of(i)), -1.0, ALU.mult, part(T["u", i], x, n_of(i)))

        def v_b(i, x):
            u = part(T["u", i], x, n_of(i))
            stt(u, u, -1.0, ALU.add, part(T["a", i], x, n_of(i)))

        def v_w(i, x):
            m = part(T["c", i], x, n_of(i))
            stt(m, part(T["r", i], x, n_of(i)), -1.0, ALU.add, m)

        def v_dp(i, x):
            q = part(T["q", i], x, 2)
            stt(q, q, -1.0, ALU.add, part(T["a", i], x, 2))

        def e_bank(i, k):
            cols = slice(k * P, (k + 1) * P)
            bank = psum_e.tile([P, PACK, P], F32, name="e")
            T["e", i, k] = bank
            nc.tensor.matmul(bank[:], lhsT=minus_ident[:], rhs=T["d", i][:, :, cols], start=True, stop=False)
            nc.tensor.matmul(bank[:], lhsT=ident[:], rhs=T["cand", i][:, :, cols], start=False, stop=True)

        def gradient(i, s, lo, hi, in0, in1):
            if ("dz", i, s) not in T:
                T["dz", i, s] = work.tile([P, BH, PACK], BF16, name="dz" + "ruc"[s], align_bytes=64)
            view = "p j (c i) -> p c j i"
            nc.vector.tensor_tensor(
                out=T["dz", i, s][:, lo:hi, :].rearrange("p (c i) j -> p c j i", i=4),
                in0=in0[:, :, lo:hi].rearrange(view, i=4),
                in1=in1.rearrange(view, i=4),
                op=ALU.mult,
            )

        def v_du(i, k):
            gradient(i, U, k * P, (k + 1) * P, T["u", i], T["e", i, k][:])

        def v_dc(i, x):
            gradient(i, C, x * HALF, (x + 1) * HALF, T["q", i], T["r", i][:, :, x * HALF : (x + 1) * HALF])

        def v_dr(i, x):
            gradient(i, R, x * HALF, (x + 1) * HALF, T["c", i], T["q", i][:, :, x * HALF : (x + 1) * HALF])

        def quant_tok(i, s):
            codes = tcode.tile([P, BH], U32, name="tok_codes", align_bytes=64)
            scales = tcode.tile([P, BH], U8, name="tok_scales", align_bytes=64)
            T["tok", i, s] = (codes, scales)
            nc.vector.quantize_mx(
                out=codes[:].bitcast(E5M2), scales=scales[:], in_=T["dz", i, s][:].rearrange("p w j -> p (w j)")
            )

        def turn(i, s, u):
            words = T["dz", i, s][:].rearrange("p w j -> p (w j)").bitcast(F32)
            bank = psum.tile([P, PACK, P], F32, name="xt")
            T["xt", i, s, u] = bank
            for t in range(PACK):
                nc.tensor.transpose(bank[:, t, :], words[:, 2 * t + u : 2 * BH : 8], ident[:])

        def regroup(i, s, u, on_vector=False):
            if ("fg", i, s) not in T:
                T["fg", i, s] = group.tile([P, 2, 2, P, PACK], BF16, name="feat_grp", align_bytes=64)
            src = T["xt", i, s, u][:].rearrange("p t q -> p (t q)").bitcast(BF16)
            copy = nc.vector.tensor_copy if on_vector else nc.scalar.copy
            copy(out=T["fg", i, s][:, u], in_=src.rearrange("p (t q e) -> p e q t", t=PACK, e=2))

        def quant_feat(i, s):
            codes = fcode.tile([P, K_PASS], U32, name="feat_codes", align_bytes=64)
            scales = fcode.tile([P, K_PASS], U8, name="feat_scales", align_bytes=64)
            T["feat", i, s] = (codes, scales)
            nc.vector.quantize_mx(
                out=codes[:].bitcast(E5M2),
                scales=scales[:],
                in_=T["fg", i, s][:].rearrange("p u e q t -> p (u e q t)"),
            )

        def turn_w(g, s, b2):
            bank = psum.tile([P, PACK, P], F32, name="xt")
            T["xw", g, s, b2] = bank
            for k in range(4):
                words = T["w", g][:, 2 * b2 + k // 2, :].bitcast(F32)
                nc.tensor.transpose(bank[:, k, :], words[:, 256 * s + k % 2 : 256 * (s + 1) : 2], ident[:])

        def regroup_w(g, s, b2):
            if ("wg", g, s) not in T:
                T["wg", g, s] = group.tile([P, BH // P, P, 2, 2], BF16, name="wh_grp", align_bytes=64)
            dst = T["wg", g, s][:].rearrange("p b o u e -> p (b o u e)").bitcast(F32)
            nc.scalar.copy(
                out=dst[:, 512 * b2 : 512 * (b2 + 1)].rearrange("p (b o u) -> p b o u", b=2, u=2),
                in_=T["xw", g, s, b2][:].rearrange("p (b u) o -> p b o u", u=2),
            )

        def quant_w(g, s):
            nc.vector.quantize_mx(
                out=w_codes[:, g, s, :].bitcast(E4M3),
                scales=w_scales[:, g, s, :],
                in_=T["wg", g, s][:].rearrange("p b o u e -> p (b o u e)"),
            )

        def group_h(g, t, x, on_vector=False):
            if ("hg", g, t) not in T:
                T["hg", g, t] = group.tile([P, BH, PACK], BF16, name="wh_grp", align_bytes=64)
            ws = slice(x * HALF, (x + 1) * HALF)
            copy = nc.vector.tensor_copy if on_vector else nc.scalar.copy
            copy(
                out=T["hg", g, t][:, ws, :].rearrange("p (c i) j -> p c j i", i=4),
                in_=T["h", g, t][:, :, ws].rearrange("p j (c i) -> p c j i", i=4),
            )

        def quant_h(g, t):
            cols = slice(g * BH, (g + 1) * BH)
            nc.vector.quantize_mx(
                out=h_codes[:, t, cols].bitcast(E4M3),
                scales=h_scales[:, t, cols],
                in_=T["hg", g, t][:].rearrange("p w j -> p (w j)"),
            )

        def drain(acc, dst, on_vector):
            res = stage.tile([P, BH], F32, name="res")
            if on_vector:
                nc.vector.tensor_copy(out=res[:], in_=acc[:])
            else:
                nc.scalar.copy(out=res[:], in_=acc[:])
            nc.sync.dma_start(out=dst, in_=res[:])

        def open_h(i, j, where):
            if where == "e":
                acc = psum_e.tile([P, BH], F32, name="e")
            elif where == "xt":
                acc = psum.tile([P, BH], F32, name="xt")
            else:
                acc = psum.tile([P, BH], F32, name="acc")
            T["acc", i, j] = acc

        def pass_h(i, j, s, start, stop):
            codes, scales = T["feat", i, s]
            g = chunks[i][0]
            nc.tensor.matmul_mx(
                out=T["acc", i, j][:],
                lhsT=codes[:, j * P : (j + 1) * P].bitcast(E5M2),
                lhsT_scale=scales[:, j * P : (j + 1) * P],
                rhs=w_codes[:, g, s, :].bitcast(E4M3),
                rhs_scale=w_scales[:, g, s, :],
                start=start,
                stop=stop,
            )

        def drain_h(i, j, on_vector=False):
            g, t = chunks[i]
            dst = out_0[rows(t), g * BH : (g + 1) * BH].rearrange("(p j) w -> p j w", j=PACK)
            drain(T["acc", i, j], dst[:, j, :], on_vector)

        def product_h(i, j):
            open_h(i, j, "acc")
            for s in (U, C, R):
                pass_h(i, j, s, s == U, s == R)

        def begin_h(i, j):
            open_h(i, j, "e" if j < 2 else "xt")
            pass_h(i, j, U, True, False)
            pass_h(i, j, C, False, False)

        def end_h(i, j):
            pass_h(i, j, R, False, True)

        def product_w(g, s, m):
            acc = psum.tile([P, BH], F32, name="acc")
            T["accw", g, s, m] = acc
            cols = slice(g * BH + m * P, g * BH + (m + 1) * P)
            for t in (0, 1):
                codes, scales = T["tok", 2 * g + t, s]
                nc.tensor.matmul_mx(
                    out=acc[:],
                    lhsT=h_codes[:, t, cols].bitcast(E4M3),
                    lhsT_scale=h_scales[:, t, cols],
                    rhs=codes[:].bitcast(E5M2),
                    rhs_scale=scales[:],
                    start=t == 0,
                    stop=t == 1,
                )

        def drain_w(g, s, m, on_vector=False):
            drain(T["accw", g, s, m], out_1[g, m * P : (m + 1) * P, s * BH : (s + 1) * BH], on_vector)

        load(0, "r", 3, 4)
        load(0, "c", 3, 4)
        sig(0, "r", 3)
        v_m(0, 3)
        tanh(0, 3)
        load_h(0, 1)
        group_h(0, 1, 1, True)
        group_h(0, 1, 0, True)
        load(0, "r", 2, 4)
        quant_h(0, 1)
        load(0, "u", 0, 4)
        sig(0, "u", 0)
        sig(0, "r", 2)
        load(0, "g", 0, 4)
        v_a(0, 0)
        load(0, "u", 1, 4)
        sig(0, "u", 1)
        load(0, "c", 2, 4)
        v_m(0, 2)
        v_b(0, 0)
        load(0, "g", 1, 4)
        v_w(0, 3)
        load(0, "u", 3, 4)
        sig(0, "u", 3)
        v_a(0, 1)
        load(0, "u", 2, 4)
        load(0, "g", 2, 4)
        sig(0, "u", 2)
        v_a(0, 2)
        load(0, "r", 0, 4)
        sig(0, "r", 0)
        load(0, "r", 1, 4)
        load(0, "g", 3, 4)
        v_b(0, 1)
        v_a(0, 3)
        tanh(0, 2)
        sig(0, "r", 1)
        load(0, "c", 0, 4)
        v_m(0, 0)
        tanh(0, 0)
        load(0, "c", 1, 4)
        v_m(0, 1)
        v_w(0, 2)
        load(0, "d")
        load_w(0)
        load_h(0, 0)
        tanh(0, 1)
        v_w(0, 0)
        square(0, 1)
        e_bank(0, 1)
        v_b(0, 3)
        square(0, 0)
        turn_w(0, 2, 1)
        regroup_w(0, 2, 1)
        turn_w(0, 2, 0)
        regroup_w(0, 2, 0)
        turn_w(0, 1, 1)
        v_b(0, 2)
        v_dp(0, 1)
        group_h(0, 0, 1)
        regroup_w(0, 1, 1)
        v_dp(0, 0)
        v_w(0, 1)
        v_dc(0, 0)
        v_dc(0, 1)
        load(1, "r")
        load(1, "c")
        sig(1, "r", 0)
        e_bank(0, 2)
        v_dr(0, 1)
        quant_w(0, 2)
        load(1, "u")
        load(1, "g")
        turn_w(0, 0, 0)
        v_du(0, 1)
        sig(1, "r", 1)
        v_du(0, 2)
        turn_w(0, 1, 0)
        e_bank(0, 3)
        v_dr(0, 0)
        turn(0, 0, 0)
        quant_tok(0, 2)
        group_h(0, 0, 0)
        v_du(0, 3)
        regroup_w(0, 0, 0)
        v_m(1, 0)
        quant_tok(0, 0)
        turn(0, 2, 0)
        regroup_w(0, 1, 0)
        v_m(1, 1)
        load_h(1, 1)
        sig(1, "u", 0)
        v_a(1, 0)
        turn_w(0, 0, 1)
        sig(1, "u", 1)
        e_bank(0, 0)
        load(1, "d")
        v_du(0, 0)
        regroup(0, 2, 0)
        regroup_w(0, 0, 1)
        quant_w(0, 1)
        v_a(1, 1)
        quant_w(0, 0)
        load_w(1)
        regroup(0, 0, 0)
        turn(0, 2, 1)
        tanh(1, 0)
        quant_tok(0, 1)
        quant_h(0, 0)
        regroup(0, 2, 1)
        v_b(1, 0)
        turn(0, 0, 1)
        turn(0, 1, 0)
        tanh(1, 1)
        square(1, 0)
        v_b(1, 1)
        turn(0, 1, 1)
        v_dp(1, 0)
        regroup(0, 1, 1)
        square(1, 1)
        load_h(1, 0)
        load(2, "d")
        e_bank(1, 1)
        regroup(0, 0, 1)
        e_bank(1, 2)
        v_du(1, 1)
        v_w(1, 0)
        v_du(1, 2)
        quant_feat(0, 2)
        v_dp(1, 1)
        regroup(0, 1, 0)
        group_h(1, 0, 1)
        e_bank(1, 0)
        load(2, "g")
        quant_feat(0, 1)
        quant_feat(0, 0)
        v_w(1, 1)
        v_dc(1, 0)
        turn_w(1, 1, 1)
        turn_w(1, 1, 0)
        regroup_w(1, 1, 0)
        load(2, "u")
        regroup_w(1, 1, 1)
        e_bank(1, 3)
        v_du(1, 3)
        product_h(0, 1)
        load(2, "r")
        load(2, "c")
        sig(2, "u", 1)
        sig(2, "r", 1)
        v_du(1, 0)
        product_h(0, 3)
        v_dc(1, 1)
        group_h(1, 0, 0)
        load(3, "r")
        load(3, "u")
        v_a(2, 1)
        turn_w(1, 0, 1)
        regroup_w(1, 0, 1)
        quant_tok(1, 1)
        sig(2, "r", 0)
        v_m(2, 0)
        product_h(0, 2)
        sig(2, "u", 0)
        drain_h(0, 2)
        v_m(2, 1)
        drain_h(0, 3)
        v_dr(1, 0)
        v_dr(1, 1)
        turn(1, 1, 1)
        drain_h(0, 1, True)
        regroup(1, 1, 1)
        tanh(2, 0)
        v_w(2, 0)
        load(3, "c")
        turn_w(1, 0, 0)
        tanh(2, 1)
        square(2, 0)
        v_b(2, 1)
        turn(1, 0, 0)
        regroup(1, 0, 0)
        product_h(0, 0)
        e_bank(2, 1)
        quant_tok(1, 0)
        regroup_w(1, 0, 0)
        turn(1, 2, 0)
        square(2, 1)
        quant_tok(1, 2)
        regroup(1, 2, 0)
        quant_w(1, 0)
        drain_h(0, 0)
        product_w(0, 1, 3)
        product_w(0, 2, 0)
        turn(1, 2, 1)
        drain_w(0, 1, 3)
        e_bank(2, 3)
        v_a(2, 0)
        v_dp(2, 1)
        turn(1, 1, 0)
        sig(3, "r", 1)
        product_w(0, 0, 0)
        quant_w(1, 1)
        v_b(2, 0)
        quant_h(1, 0)
        drain_w(0, 2, 0)
        load(3, "g")
        v_du(2, 1)
        v_dp(2, 0)
        load(3, "d")
        turn(1, 0, 1)
        regroup(1, 2, 1)
        regroup(1, 1, 0)
        turn_w(1, 2, 0)
        drain_w(0, 0, 0)
        e_bank(2, 2)
        turn_w(1, 2, 1)
        sig(3, "r", 0)
        quant_feat(1, 2)
        sig(3, "u", 0)
        group_h(1, 1, 0)
        regroup(1, 0, 1)
        regroup_w(1, 2, 1)
        v_dc(2, 1)
        v_du(2, 3)
        v_dc(2, 0)
        quant_feat(1, 1)
        e_bank(2, 0)
        v_w(2, 1)
        quant_feat(1, 0)
        v_dr(2, 1)
        product_w(0, 0, 3)
        drain_w(0, 0, 3)
        product_w(0, 1, 0)
        v_dr(2, 0)
        v_a(3, 0)
        regroup_w(1, 2, 0)
        product_h(1, 1)
        v_du(2, 0)
        v_m(3, 0)
        sig(3, "u", 1)
        product_h(1, 0)
        drain_w(0, 1, 0)
        drain_h(1, 0)
        turn(2, 2, 1)
        drain_h(1, 1)
        turn(2, 0, 1)
        v_du(2, 2)
        product_w(0, 1, 1)
        turn(2, 0, 0)
        product_h(1, 2)
        regroup(2, 2, 1)
        regroup(2, 0, 1)
        turn(2, 2, 0)
        turn(2, 1, 1)
        regroup(2, 0, 0)
        product_h(1, 3)
        v_m(3, 1)
        tanh(3, 0)
        drain_w(0, 1, 1)
        tanh(3, 1)
        drain_h(1, 3)
        quant_tok(2, 1)
        drain_h(1, 2)
        square(3, 1)
        turn(2, 1, 0)
        product_w(0, 0, 2)
        e_bank(3, 0)
        regroup(2, 1, 1)
        regroup(2, 1, 0)
        regroup(2, 2, 0)
        e_bank(3, 2)
        v_a(3, 1)
        v_b(3, 0)
        v_b(3, 1)
        drain_w(0, 0, 2)
        v_w(3, 1)
        v_du(3, 0)
        quant_w(1, 2)
        product_w(0, 2, 2)
        drain_w(0, 2, 2)
        v_du(3, 2)
        product_w(0, 2, 3)
        drain_w(0, 2, 3)
        group_h(1, 1, 1, True)
        e_bank(3, 3)
        e_bank(3, 1)
        product_w(0, 1, 2)
        quant_feat(2, 0)
        quant_feat(2, 1)
        v_du(3, 3)
        quant_feat(2, 2)
        v_du(3, 1)
        square(3, 0)
        product_h(2, 1)
        turn(3, 1, 1)
        drain_w(0, 1, 2)
        drain_h(2, 1)
        quant_h(1, 1)
        quant_tok(3, 1)
        product_h(2, 0)
        drain_h(2, 0)
        product_w(0, 2, 1)
        v_dp(3, 0)
        drain_w(0, 2, 1)
        product_w(1, 1, 2)
        v_dp(3, 1)
        quant_tok(2, 2)
        drain_w(1, 1, 2)
        product_w(0, 0, 1)
        product_w(1, 1, 1)
        drain_w(0, 0, 1)
        product_w(1, 1, 0)
        v_dc(3, 1)
        product_h(2, 2)
        drain_w(1, 1, 1)
        regroup(3, 1, 1)
        drain_h(2, 2)
        drain_w(1, 1, 0)
        product_h(2, 3)
        v_dc(3, 0)
        turn(3, 2, 1)
        turn(3, 1, 0)
        regroup(3, 2, 1)
        turn(3, 2, 0)
        v_w(3, 0)
        quant_tok(3, 2)
        drain_h(2, 3)
        quant_tok(2, 0)
        product_w(1, 2, 2)
        drain_w(1, 2, 2)
        v_dr(3, 0)
        v_dr(3, 1)
        product_w(1, 2, 0)
        drain_w(1, 2, 0)
        regroup(3, 2, 0)
        regroup(3, 1, 0, True)
        product_w(1, 1, 3)
        drain_w(1, 1, 3)
        product_w(1, 2, 1)
        product_w(1, 2, 3)
        turn(3, 0, 0)
        turn(3, 0, 1)
        quant_tok(3, 0)
        quant_feat(3, 2)
        quant_feat(3, 1)
        drain_w(1, 2, 3)
        drain_w(1, 2, 1)
        regroup(3, 0, 0)
        regroup(3, 0, 1, True)
        product_w(1, 0, 1)
        quant_feat(3, 0)
        drain_w(1, 0, 1)
        product_w(1, 0, 0)
        drain_w(1, 0, 0)
        begin_h(3, 0)
        product_w(1, 0, 2)
        drain_w(1, 0, 2, True)
        begin_h(3, 3)
        end_h(3, 0)
        end_h(3, 3)
        drain_h(3, 0)
        product_w(1, 0, 3)
        drain_h(3, 3)
        begin_h(3, 2)
        end_h(3, 2)
        drain_w(1, 0, 3)
        drain_h(3, 2)
        begin_h(3, 1)
        end_h(3, 1)
        drain_h(3, 1)
